import numpy as np
import ml_dtypes


def mxq(x, axis, fmt="e4m3"):
    dtype, down = {"e4m3": (ml_dtypes.float8_e4m3fn, 7), "e5m2": (ml_dtypes.float8_e5m2, 14)}[fmt]
    v = np.moveaxis(np.asarray(x, np.float32).astype(ml_dtypes.bfloat16).astype(np.float64), axis, -1)
    blocks = v.reshape(v.shape[:-1] + (-1, 32))
    amax = np.abs(blocks).max(-1, keepdims=True)
    byte = np.maximum(np.where(amax > 0, np.frexp(amax)[1] - 1 + 127, 0) - down, 1)
    scale = np.exp2(byte - 127.0)
    codes = (blocks / scale).astype(np.float32).astype(dtype).astype(np.float64)
    return np.moveaxis((codes * scale).reshape(v.shape), -1, axis)


WIDE = False


def mx_kscale(k):
    if not WIDE:
        return np.ones(k)
    levels = np.array([10, -10, 5, -5, 0])
    if k % 512:
        return np.exp2(np.random.permutation(np.resize(levels, k // 32))).repeat(32)
    a = np.empty((k // 512, 16))
    for p in range(k // 512):
        a[p, :8] = np.random.permutation(np.resize(levels, 8))
        for g in range(8):
            far = levels[np.abs(levels - a[p, g]) >= 10]
            a[p, g + 8] = far[np.random.randint(len(far))]
    return np.exp2(a.ravel()).repeat(32)


BF16 = ml_dtypes.bfloat16


def bf(x):
    return np.asarray(x, np.float32).astype(BF16)


def f64(x):
    return np.asarray(x).astype(np.float64)


B, H, L, D, C = 8, 4, 512, 128, 512


def decay_block(i0, n):
    head_idx = np.arange(H, dtype=np.float64)
    gamma = 1.0 - np.exp2(-5.0 - head_idx)
    log2_gamma = np.log2(gamma)
    pos_diff = np.arange(i0, i0 + C, dtype=np.float64)[:, None] - np.arange(n, dtype=np.float64)[None, :]
    causal = np.where(pos_diff >= 0, 1.0, 0.0)
    return np.exp2(pos_diff[None] * log2_gamma[:, None, None]) * causal[None]


def setup_inputs():
    s = mx_kscale(L)
    return {"q_scaled": bf(np.random.standard_normal((B, H, L, D)) / np.sqrt(D)),
            "k": bf(np.random.standard_normal((B, H, L, D)) * s[:, None]),
            "v": bf(np.random.standard_normal((B, H, L, D)) * 0.25 / s[:, None])}


def reference(q_scaled, k, v):
    vq = mxq(f64(v), 2, "e4m3")
    out = np.zeros((B, H, L, D))
    for i0 in range(0, L, C):
        n = i0 + C
        scores = f64(q_scaled)[:, :, i0:n] @ f64(k)[:, :, :n].transpose(0, 1, 3, 2)
        p = scores * decay_block(i0, n)[None]
        out[:, :, i0:n] = mxq(p, 3, "e4m3") @ vq[:, :, :n]
    return out

@@ -1,0 +1,218 @@
+import math
+from contextlib import ExitStack
+
+import concourse.mybir as mybir
+from concourse.masks import make_identity
+
+B, H, L, D = 8, 4, 512, 128
+P = 128
+NH = B * H
+FLOPS = 4 * B * H * L * L * D
+
+BF16 = mybir.dt.bfloat16
+F32 = mybir.dt.float32
+U32 = mybir.dt.uint32
+U8 = mybir.dt.uint8
+FP8X4 = mybir.dt.float8_e4m3fn_x4
+ALU = mybir.AluOpType
+ACT = mybir.ActivationFunctionType
+
+FAR = 131072.0
+NG = 2
+AHEAD = 3
+ON_G = (0,)
+
+
+def tile_model_pa_t_kernel(tc, q_scaled, k, v, out):
+    nc = tc.nc
+    with ExitStack() as ctx:
+        ctx.enter_context(tc.manual_schedule())
+        const = ctx.enter_context(tc.tile_pool(name="const", bufs=1))
+        inp = ctx.enter_context(tc.tile_pool(name="inp", bufs=1))
+        work = ctx.enter_context(tc.tile_pool(name="work", bufs=3))
+        outp = ctx.enter_context(tc.tile_pool(name="outp", bufs=4))
+        pt = ctx.enter_context(tc.psum_pool(name="pt", bufs=2))
+        ps = ctx.enter_context(tc.psum_pool(name="ps", bufs=4))
+        po = ctx.enter_context(tc.psum_pool(name="po", bufs=2))
+
+        q_sb, k_sb, v_sb = [], [], []
+        for b in range(B):
+            q_sb.append(inp.tile([P, H, 4 * D], BF16, name="q_sb%d" % b))
+            k_sb.append(inp.tile([P, H, 4 * D], BF16, name="k_sb%d" % b))
+            v_sb.append(inp.tile([P, H, 4 * D], BF16, name="v_sb%d" % b))
+
+        def load(b):
+            cuts = [(0, 1), (1, H)] if b == 0 else [(0, H)]
+            for h0, h1 in cuts:
+                nc.sync.dma_start(
+                    out=q_sb[b][:, h0:h1, :],
+                    in_=q_scaled[b, h0:h1].rearrange("h (m u) d -> m h (u d)", u=4),
+                )
+                nc.sync.dma_start(
+                    out=k_sb[b][:, h0:h1, :],
+                    in_=k[b, h0:h1].rearrange("h (p t) d -> p h (t d)", t=4),
+                )
+                nc.sync.dma_start(
+                    out=v_sb[b][:, h0:h1, :],
+                    in_=v[b, h0:h1].rearrange("h (p t) d -> p h (t d)", t=4),
+                )
+
+        for b in range(AHEAD):
+            load(b)
+
+        ident = const.tile([P, P], BF16, name="ident")
+        make_identity(nc, ident[:])
+        expo = const.tile([P, 4, 512], F32, name="expo")
+        for ib in range(4):
+            nc.gpsimd.iota(
+                expo[:, ib, :],
+                pattern=[[1, 4], [4, 32], [-1, 4]],
+                base=128 * ib,
+                channel_multiplier=-4,
+                allow_small_or_imprecise_dtypes=True,
+            )
+            nc.gpsimd.affine_select(
+                out=expo[:, ib, :],
+                in_=expo[:, ib, :],
+                pattern=[[1, 4], [4, 32], [-1, 4]],
+                compare_op=ALU.is_ge,
+                fill=FAR,
+                base=128 * ib,
+                channel_multiplier=-4,
+            )
+        g_tiles = []
+        for i in range(NG):
+            g = const.tile([P, 2048], BF16, name="g%d" % i, align_bytes=64)
+            g_tiles.append(g)
+        tabs = {}
+
+        def build_table(h):
+            tab = const.tile([P, 4, 512], F32, name="tab%d" % h)
+            nc.scalar.activation(out=tab[:], in_=expo[:], func=ACT.Exp, scale=math.log(1.0 - 2.0 ** (-5 - h)))
+            tabs[h] = tab
+
+        qkT, s_ps, fed, words, planes, vwords, vplanes, vgs = {}, {}, {}, {}, {}, {}, {}, {}
+
+        def transposes(n):
+            b, h = divmod(n, H)
+            t_ps = pt.tile([P, 1024], BF16, name="t_ps")
+            for u in range(4):
+                nc.tensor.transpose(t_ps[:, 128 * u : 128 * u + 128], q_sb[b][:, h, 128 * u : 128 * u + 128], ident[:])
+            for t in range(4):
+                nc.tensor.transpose(t_ps[:, 512 + 128 * t : 640 + 128 * t], k_sb[b][:, h, 128 * t : 128 * t + 128], ident[:])
+            qk = work.tile([P, 1024], BF16, name="qk")
+            nc.scalar.copy(out=qk[:], in_=t_ps[:])
+            qkT[n] = qk
+
+        def regroup_v(n):
+            b, h = divmod(n, H)
+            if h == 0:
+                vg_new = work.tile([P, H, 512], BF16, name="vg", align_bytes=64, bufs=2)
+                vgs[b] = vg_new
+            nc.scalar.copy(
+                out=vgs[b][:, h, :].rearrange("p (c i t) -> p c t i", i=4, t=4),
+                in_=v_sb[b][:, h, :].rearrange("p (t c i) -> p c t i", t=4, i=4),
+            )
+
+        def quantise_v(b):
+            vw = work.tile([P, H, 128], U32, name="vw", align_bytes=64, bufs=3)
+            vp = work.tile([P, H, 128], U8, name="vp", align_bytes=64, bufs=3)
+            nc.vector.quantize_mx(
+                out=vw[:].rearrange("p h c -> p (h c)").bitcast(FP8X4),
+                scales=vp[:].rearrange("p h c -> p (h c)"),
+                in_=vgs[b][:].rearrange("p h c -> p (h c)"),
+            )
+            vwords[b], vplanes[b] = vw, vp
+
+        def scores(n):
+            qk = qkT[n]
+            tiles = []
+            for ib in range(4):
+                s = ps.tile([P, 4, 128], F32, name="s_ps")
+                tiles.append(s)
+            s_ps[n] = tiles
+            qv = qk[:, 0:512].rearrange("d (u m) -> d u m", u=4)
+            for ib in (2, 3, 1, 0):
+                for t in range(4):
+                    nc.tensor.matmul(
+                        out=tiles[ib][:, t, :].rearrange("p (u m) -> p u m", u=4),
+                        lhsT=qk[:, 512 + 128 * t : 640 + 128 * t],
+                        rhs=qv[:, :, 32 * ib : 32 * ib + 32],
+                        start=True,
+                        stop=True,
+                    )
+
+        def feed(n, ib):
+            f = work.tile([P, 4, 128], F32, name="fed%d" % ib)
+            nc.scalar.copy(out=f[:], in_=s_ps[n][ib][:])
+            fed[(n, ib)] = f
+
+        def decay(n, ib):
+            h = n % H
+            gv = g_tiles[n % NG][:].rearrange("p (u m t) -> p u m t", u=4, t=4)
+            if ib in ON_G:
+                eng, src = nc.gpsimd, fed[(n, ib)][:]
+            else:
+                eng, src = nc.vector, s_ps[n][ib][:]
+            eng.tensor_tensor(
+                out=gv[:, :, 32 * ib : 32 * ib + 32, :],
+                in0=src.rearrange("p t (u m) -> p u m t", u=4),
+                in1=tabs[h][:, ib, :].rearrange("p (u m t) -> p u m t", u=4, t=4),
+                op=ALU.mult,
+            )
+
+        def quantise_p(n):
+            w = work.tile([P, 512], U32, name="w", align_bytes=64, bufs=4)
+            pl = work.tile([P, 512], U8, name="pl", align_bytes=64, bufs=4)
+            nc.vector.quantize_mx(out=w[:].bitcast(FP8X4), scales=pl[:], in_=g_tiles[n % NG][:])
+            words[n], planes[n] = w, pl
+
+        def second_matmul(n):
+            b, h = divmod(n, H)
+            o_ps = po.tile([P, 512], F32, name="o_ps")
+            for u in range(4):
+                cols = slice(128 * u, 128 * u + 128)
+                nc.tensor.matmul_mx(
+                    out=o_ps[:, cols],
+                    lhsT=words[n][:, cols].bitcast(FP8X4),
+                    lhsT_scale=planes[n][:, cols],
+                    rhs=vwords[b][:, h, :].bitcast(FP8X4),
+                    rhs_scale=vplanes[b][:, h, :],
+                    start=True,
+                    stop=True,
+                )
+            o_sb = outp.tile([P, 512], F32, name="o_sb")
+            nc.scalar.copy(out=o_sb[:], in_=o_ps[:])
+            nc.sync.dma_start(out=out[b, h].rearrange("(m u) d -> m (u d)", u=4), in_=o_sb[:])
+
+        def live(n):
+            return 0 <= n < NH
+
+        REGROUP = {2: (2,), 3: (2, 3), 0: (3,), 1: ()}
+
+        for it in range(-2, NH + 2):
+            if it >= 0 and it % H == 0 and it // H + AHEAD < B:
+                load(it // H + AHEAD)
+            if live(it - 2):
+                second_matmul(it - 2)
+            if live(it + 2):
+                transposes(it + 2)
+                if it + 2 < H:
+                    build_table(it + 2)
+            if live(it + 1):
+                scores(it + 1)
+                for ib in ON_G:
+                    feed(it + 1, ib)
+            for ahead in REGROUP[it % 4]:
+                if live(it + ahead):
+                    regroup_v(it + ahead)
+            if live(it):
+                decay(it, 2)
+                decay(it, 3)
+            if it % H == 1 and live(it):
+                quantise_v(it // H)
+            if live(it - 1):
+                quantise_p(it - 1)
+            if live(it):
+                decay(it, 1)
+                decay(it, 0)

@@ -6,11 +6,12 @@ from concourse.masks import make_identity
 
 B, H, L, D = 8, 4, 512, 128
 P = 128
-NH = B * H
+NP = B * H // 2
 FLOPS = 4 * B * H * L * L * D
 
 BF16 = mybir.dt.bfloat16
 F32 = mybir.dt.float32
+I32 = mybir.dt.int32
 U32 = mybir.dt.uint32
 U8 = mybir.dt.uint8
 FP8X4 = mybir.dt.float8_e4m3fn_x4
@@ -18,9 +19,14 @@ ALU = mybir.AluOpType
 ACT = mybir.ActivationFunctionType
 
 FAR = 131072.0
-NG = 2
-AHEAD = 3
-ON_G = (0,)
+
+KINDS = {"A3": ((0, 3),), "B3": ((1, 3),), "X": ((0, 2), (1, 0)), "Y": ((1, 2), (0, 0)), "Z": ((0, 1), (1, 1))}
+ORDER = ("A3", "B3", "X", "Y", "Z")
+SLOT = {kind: i for i, kind in enumerate(ORDER)}
+
+
+def group_of(head, kg):
+    return kg if head == 0 else 3 - kg
 
 
 def tile_model_pa_t_kernel(tc, q_scaled, k, v, out):
@@ -30,189 +36,254 @@ def tile_model_pa_t_kernel(tc, q_scaled, k, v, out):
         const = ctx.enter_context(tc.tile_pool(name="const", bufs=1))
         inp = ctx.enter_context(tc.tile_pool(name="inp", bufs=1))
         work = ctx.enter_context(tc.tile_pool(name="work", bufs=3))
-        outp = ctx.enter_context(tc.tile_pool(name="outp", bufs=4))
+        outp = ctx.enter_context(tc.tile_pool(name="outp", bufs=3))
         pt = ctx.enter_context(tc.psum_pool(name="pt", bufs=2))
         ps = ctx.enter_context(tc.psum_pool(name="ps", bufs=4))
-        po = ctx.enter_context(tc.psum_pool(name="po", bufs=2))
+        po = ctx.enter_context(tc.psum_pool(name="po", bufs=1))
 
-        q_sb, k_sb, v_sb = [], [], []
-        for b in range(B):
-            q_sb.append(inp.tile([P, H, 4 * D], BF16, name="q_sb%d" % b))
-            k_sb.append(inp.tile([P, H, 4 * D], BF16, name="k_sb%d" % b))
-            v_sb.append(inp.tile([P, H, 4 * D], BF16, name="v_sb%d" % b))
+        k_by_side = k.rearrange("(i s) h l d -> s h i l d", s=2)
+        v_by_side = v.rearrange("(i s) h l d -> s h i l d", s=2)
+        place = {}
 
-        def load(b):
-            cuts = [(0, 1), (1, H)] if b == 0 else [(0, H)]
-            for h0, h1 in cuts:
-                nc.sync.dma_start(
-                    out=q_sb[b][:, h0:h1, :],
-                    in_=q_scaled[b, h0:h1].rearrange("h (m u) d -> m h (u d)", u=4),
-                )
-                nc.sync.dma_start(
-                    out=k_sb[b][:, h0:h1, :],
-                    in_=k[b, h0:h1].rearrange("h (p t) d -> p h (t d)", t=4),
-                )
-                nc.sync.dma_start(
-                    out=v_sb[b][:, h0:h1, :],
-                    in_=v[b, h0:h1].rearrange("h (p t) d -> p h (t d)", t=4),
-                )
+        def load(n0, n1):
+            h, i0 = divmod(n0, 4)
+            i1 = i0 + n1 - n0
+            ni = n1 - n0
+            q_sb = inp.tile([P, 2 * ni, 4 * D], BF16, name="q_sb%d" % n0)
+            k_sb = inp.tile([P, 2, ni, 4 * D], BF16, name="k_sb%d" % n0)
+            v_sb = inp.tile([P, 2, ni, 4 * D], BF16, name="v_sb%d" % n0)
+            nc.sync.dma_start(out=q_sb[:], in_=q_scaled[2 * i0 : 2 * i1, h].rearrange("b (m u) d -> m b (u d)", u=4))
+            for dst, src in ((k_sb, k_by_side), (v_sb, v_by_side)):
+                nc.sync.dma_start(out=dst[:, 0], in_=src[0, h, i0:i1].rearrange("i (p t) d -> p i (t d)", t=4))
+                for kg in range(4):
+                    g = group_of(1, kg)
+                    nc.sync.dma_start(
+                        out=dst[32 * g : 32 * g + 32, 1],
+                        in_=src[1, h, i0:i1, 128 * kg : 128 * kg + 128].rearrange("i (p t) d -> p i (t d)", t=4),
+                    )
+            for j in range(ni):
+                place[n0 + j] = (q_sb, k_sb, v_sb, j)
 
-        for b in range(AHEAD):
-            load(b)
+        GROUPS = [(0, 1), (1, 2), (2, 4)] + [(n, n + 2) for n in range(4, NP, 2)]
+        for n0, n1 in GROUPS[:4]:
+            load(n0, n1)
+
+        shift = const.tile([P, 5], F32, name="shift")
+        for kind in ORDER:
+            vals = [0] * 4
+            for head, qb in KINDS[kind]:
+                for kg in range(qb + 1):
+                    g = group_of(head, kg)
+                    vals[g] = float(128 * (g + qb - kg))
+            col = shift[:, SLOT[kind] : SLOT[kind] + 1]
+            for g in range(4):
+                nc.vector.memset(col[32 * g : 32 * g + 32, :], vals[g])
 
         ident = const.tile([P, P], BF16, name="ident")
         make_identity(nc, ident[:])
-        expo = const.tile([P, 4, 512], F32, name="expo")
-        for ib in range(4):
-            nc.gpsimd.iota(
-                expo[:, ib, :],
-                pattern=[[1, 4], [4, 32], [-1, 4]],
-                base=128 * ib,
-                channel_multiplier=-4,
-                allow_small_or_imprecise_dtypes=True,
+        expo0 = const.tile([P, 512], F32, name="expo0")
+        nc.gpsimd.iota(
+            expo0[:], pattern=[[1, 128], [-1, 4]], base=0, channel_multiplier=-4, allow_small_or_imprecise_dtypes=True
+        )
+        expo = const.tile([P, 5, 512], F32, name="expo")
+        for kind in ORDER:
+            i = SLOT[kind]
+            behind = work.tile([P, 512], F32, name="behind")
+            nc.vector.tensor_scalar(
+                out=behind[:], in0=expo0[:], scalar1=shift[:, i : i + 1], scalar2=0.0, op0=ALU.add, op1=ALU.is_lt
             )
-            nc.gpsimd.affine_select(
-                out=expo[:, ib, :],
-                in_=expo[:, ib, :],
-                pattern=[[1, 4], [4, 32], [-1, 4]],
-                compare_op=ALU.is_ge,
-                fill=FAR,
-                base=128 * ib,
-                channel_multiplier=-4,
+            ahead = work.tile([P, 512], F32, name="ahead")
+            nc.vector.tensor_scalar_add(out=ahead[:], in0=expo0[:], scalar1=shift[:, i : i + 1])
+            nc.vector.scalar_tensor_tensor(
+                out=expo[:, i, :], in0=behind[:], scalar=FAR, in1=ahead[:], op0=ALU.mult, op1=ALU.max
             )
-        g_tiles = []
-        for i in range(NG):
-            g = const.tile([P, 2048], BF16, name="g%d" % i, align_bytes=64)
-            g_tiles.append(g)
         tabs = {}
 
-        def build_table(h):
-            tab = const.tile([P, 4, 512], F32, name="tab%d" % h)
-            nc.scalar.activation(out=tab[:], in_=expo[:], func=ACT.Exp, scale=math.log(1.0 - 2.0 ** (-5 - h)))
-            tabs[h] = tab
+        def build_table(h, kind):
+            i = SLOT[kind]
+            if i == 0:
+                tab = const.tile([P, 5, 512], F32, name="tab%d" % h)
+                tabs[h] = tab
+            nc.scalar.activation(
+                out=tabs[h][:, i, :], in_=expo[:, i, :], func=ACT.Exp, scale=math.log(1.0 - 2.0 ** (-5 - h))
+            )
 
-        qkT, s_ps, fed, words, planes, vwords, vplanes, vgs = {}, {}, {}, {}, {}, {}, {}, {}
+        kz, vp, vz = [], [], []
+        for i in range(2):
+            for s in range(2):
+                t = const.tile([P, 4, 4, 128], BF16, name="kz%d%d" % (i, s))
+                nc.gpsimd.memset(t[:, 1:4].rearrange("p v t c -> p (v t c)").bitcast(I32), 0)
+                kz.append(t)
+            p_full = const.tile([P, 2, 128], U8, name="vp%d" % i, align_bytes=64)
+            nc.vector.memset(p_full[:].rearrange("p s c -> p (s c)").bitcast(I32), 0)
+            vp.append(p_full)
+            p_part = const.tile([P, 3, 2, 128], U8, name="vz%d" % i, align_bytes=64)
+            nc.gpsimd.memset(p_part[:].rearrange("p k s c -> p (k s c)").bitcast(I32), 0)
+            vz.append(p_part)
+
+        qT, s_ps, grouped, words, planes, vgs, vwords = {}, {}, {}, {}, {}, {}, {}
 
         def transposes(n):
-            b, h = divmod(n, H)
-            t_ps = pt.tile([P, 1024], BF16, name="t_ps")
-            for u in range(4):
-                nc.tensor.transpose(t_ps[:, 128 * u : 128 * u + 128], q_sb[b][:, h, 128 * u : 128 * u + 128], ident[:])
-            for t in range(4):
-                nc.tensor.transpose(t_ps[:, 512 + 128 * t : 640 + 128 * t], k_sb[b][:, h, 128 * t : 128 * t + 128], ident[:])
-            qk = work.tile([P, 1024], BF16, name="qk")
-            nc.scalar.copy(out=qk[:], in_=t_ps[:])
-            qkT[n] = qk
-
-        def regroup_v(n):
-            b, h = divmod(n, H)
-            if h == 0:
-                vg_new = work.tile([P, H, 512], BF16, name="vg", align_bytes=64, bufs=2)
-                vgs[b] = vg_new
-            nc.scalar.copy(
-                out=vgs[b][:, h, :].rearrange("p (c i t) -> p c t i", i=4, t=4),
-                in_=v_sb[b][:, h, :].rearrange("p (t c i) -> p c t i", t=4, i=4),
-            )
-
-        def quantise_v(b):
-            vw = work.tile([P, H, 128], U32, name="vw", align_bytes=64, bufs=3)
-            vp = work.tile([P, H, 128], U8, name="vp", align_bytes=64, bufs=3)
-            nc.vector.quantize_mx(
-                out=vw[:].rearrange("p h c -> p (h c)").bitcast(FP8X4),
-                scales=vp[:].rearrange("p h c -> p (h c)"),
-                in_=vgs[b][:].rearrange("p h c -> p (h c)"),
-            )
-            vwords[b], vplanes[b] = vw, vp
-
-        def scores(n):
-            qk = qkT[n]
-            tiles = []
-            for ib in range(4):
-                s = ps.tile([P, 4, 128], F32, name="s_ps")
-                tiles.append(s)
-            s_ps[n] = tiles
-            qv = qk[:, 0:512].rearrange("d (u m) -> d u m", u=4)
-            for ib in (2, 3, 1, 0):
+            q_sb, k_sb, v_sb, j = place[n]
+            for s in range(2):
+                t_ps = pt.tile([P, 1024], BF16, name="t_ps")
                 for t in range(4):
+                    nc.tensor.transpose(
+                        t_ps[:, 128 * t : 128 * t + 128], k_sb[:, s, j, 128 * t : 128 * t + 128], ident[:]
+                    )
+                for u in range(4):
+                    nc.tensor.transpose(
+                        t_ps[:, 512 + 128 * u : 640 + 128 * u], q_sb[:, 2 * j + s, 128 * u : 128 * u + 128], ident[:]
+                    )
+                nc.scalar.copy(out=kz[2 * (n % 2) + s][:, 0].rearrange("p t c -> p (t c)"), in_=t_ps[:, 0:512])
+                q_t = work.tile([P, 512], BF16, name="q_t%d" % s)
+                nc.scalar.copy(out=q_t[:], in_=t_ps[:, 512:1024])
+                qT[(n, s)] = q_t
+
+        def mask_keys(n):
+            for s in range(2):
+                t = kz[2 * (n % 2) + s]
+                for z in range(1, 4):
+                    cols = slice(0, 128 - 32 * z) if s == 0 else slice(32 * z, 128)
+                    nc.gpsimd.tensor_copy(out=t[:, z, :, cols], in_=t[:, 0, :, cols])
+
+        def scores(n, kind):
+            s_tile = ps.tile([P, 4, 128], F32, name="s_ps")
+            s_ps[(n, kind)] = s_tile
+            parts = KINDS[kind]
+            for t in range(4):
+                for i, (head, qb) in enumerate(parts):
                     nc.tensor.matmul(
-                        out=tiles[ib][:, t, :].rearrange("p (u m) -> p u m", u=4),
-                        lhsT=qk[:, 512 + 128 * t : 640 + 128 * t],
-                        rhs=qv[:, :, 32 * ib : 32 * ib + 32],
-                        start=True,
-                        stop=True,
+                        out=s_tile[:, t, :].rearrange("p (u m) -> p u m", u=4),
+                        lhsT=kz[2 * (n % 2) + head][:, 3 - qb, t, :],
+                        rhs=qT[(n, head)][:].rearrange("d (u m) -> d u m", u=4)[:, :, 32 * qb : 32 * qb + 32],
+                        start=i == 0,
+                        stop=i == len(parts) - 1,
                     )
 
-        def feed(n, ib):
-            f = work.tile([P, 4, 128], F32, name="fed%d" % ib)
-            nc.scalar.copy(out=f[:], in_=s_ps[n][ib][:])
-            fed[(n, ib)] = f
-
-        def decay(n, ib):
-            h = n % H
-            gv = g_tiles[n % NG][:].rearrange("p (u m t) -> p u m t", u=4, t=4)
-            if ib in ON_G:
-                eng, src = nc.gpsimd, fed[(n, ib)][:]
-            else:
-                eng, src = nc.vector, s_ps[n][ib][:]
-            eng.tensor_tensor(
-                out=gv[:, :, 32 * ib : 32 * ib + 32, :],
-                in0=src.rearrange("p t (u m) -> p u m t", u=4),
-                in1=tabs[h][:, ib, :].rearrange("p (u m t) -> p u m t", u=4, t=4),
+        def decay(n, kind):
+            i = SLOT[kind]
+            if i == 0:
+                g_new = work.tile([P, 5, 512], BF16, name="grouped", align_bytes=64, bufs=2)
+                grouped[n] = g_new
+            nc.vector.tensor_tensor(
+                out=grouped[n][:, i, :].rearrange("p (m u t) -> p m u t", u=4, t=4),
+                in0=s_ps[(n, kind)][:].rearrange("p t (u m) -> p m u t", u=4),
+                in1=tabs[n // 4][:, i, :].rearrange("p (m u t) -> p m u t", u=4, t=4),
                 op=ALU.mult,
             )
 
-        def quantise_p(n):
-            w = work.tile([P, 512], U32, name="w", align_bytes=64, bufs=4)
-            pl = work.tile([P, 512], U8, name="pl", align_bytes=64, bufs=4)
-            nc.vector.quantize_mx(out=w[:].bitcast(FP8X4), scales=pl[:], in_=g_tiles[n % NG][:])
-            words[n], planes[n] = w, pl
+        def quantise_p(n, part):
+            if part == 0:
+                w_new = work.tile([P, 5, 128], U32, name="w", align_bytes=64)
+                pl_new = work.tile([P, 5, 128], U8, name="pl", align_bytes=64)
+                words[n], planes[n] = w_new, pl_new
+            sel = slice(0, 4) if part == 0 else slice(4, 5)
+            nc.vector.quantize_mx(
+                out=words[n][:, sel, :].rearrange("p k c -> p (k c)").bitcast(FP8X4),
+                scales=planes[n][:, sel, :].rearrange("p k c -> p (k c)"),
+                in_=grouped[n][:, sel, :].rearrange("p k c -> p (k c)"),
+            )
+
+        def regroup_v(n, s):
+            q_sb, k_sb, v_sb, j = place[n]
+            if s == 0:
+                vg_new = work.tile([P, 2, 512], BF16, name="vg", align_bytes=64, bufs=2)
+                vgs[n] = vg_new
+            nc.scalar.copy(
+                out=vgs[n][:, s, :].rearrange("p (c i t) -> p c t i", i=4, t=4),
+                in_=v_sb[:, s, j, :].rearrange("p (t c i) -> p c t i", t=4, i=4),
+            )
+
+        def quantise_v(n):
+            vw = work.tile([P, 2, 128], U32, name="vw", align_bytes=64)
+            vwords[n] = vw
+            nc.vector.quantize_mx(
+                out=vw[:].rearrange("p s c -> p (s c)").bitcast(FP8X4),
+                scales=vp[n % 2][:].rearrange("p s c -> p (s c)"),
+                in_=vgs[n][:].rearrange("p s c -> p (s c)"),
+            )
+
+        def mask_values(n):
+            full, part = vp[n % 2], vz[n % 2]
+            for i, kind in enumerate(("X", "Y", "Z")):
+                for head, qb in KINDS[kind]:
+                    lo, hi = (0, 32 * qb + 32) if head == 0 else (96 - 32 * qb, 128)
+                    cuts = [(lo, hi)] if (lo, hi) != (32, 128) else [(32, 64), (64, 128)]
+                    for a, b in cuts:
+                        nc.gpsimd.tensor_copy(
+                            out=part[a:b, i, head, :].bitcast(I32), in_=full[a:b, head, :].bitcast(I32)
+                        )
 
         def second_matmul(n):
-            b, h = divmod(n, H)
-            o_ps = po.tile([P, 512], F32, name="o_ps")
-            for u in range(4):
-                cols = slice(128 * u, 128 * u + 128)
+            h, i = divmod(n, 4)
+            low = po.tile([P, 4, 128], F32, name="o_low")
+            high = po.tile([P, 4, 128], F32, name="o_high")
+
+            def multiply(dst, kind, rhs, rhs_scale):
                 nc.tensor.matmul_mx(
-                    out=o_ps[:, cols],
-                    lhsT=words[n][:, cols].bitcast(FP8X4),
-                    lhsT_scale=planes[n][:, cols],
-                    rhs=vwords[b][:, h, :].bitcast(FP8X4),
-                    rhs_scale=vplanes[b][:, h, :],
+                    out=dst.rearrange("p j d -> p (j d)"),
+                    lhsT=words[n][:, SLOT[kind], :].bitcast(FP8X4),
+                    lhsT_scale=planes[n][:, SLOT[kind], :],
+                    rhs=rhs.rearrange("p s c -> p (s c)").bitcast(FP8X4),
+                    rhs_scale=rhs_scale.rearrange("p s c -> p (s c)"),
                     start=True,
                     stop=True,
                 )
-            o_sb = outp.tile([P, 512], F32, name="o_sb")
-            nc.scalar.copy(out=o_sb[:], in_=o_ps[:])
-            nc.sync.dma_start(out=out[b, h].rearrange("(m u) d -> m (u d)", u=4), in_=o_sb[:])
+
+            vw = vwords[n]
+            multiply(low[:, 2:3, :], "A3", vw[:, 0:1, :], vp[n % 2][:, 0:1, :])
+            multiply(low[:, 3:4, :], "B3", vw[:, 1:2, :], vp[n % 2][:, 1:2, :])
+            multiply(low[:, 0:2, :], "Z", vw[:], vz[n % 2][:, 2])
+            multiply(high[:, 0:2, :], "X", vw[:], vz[n % 2][:, 0])
+            multiply(high[:, 2:4, :], "Y", vw[:], vz[n % 2][:, 1])
+            o_sb = outp.tile([P, 2, 4, 128], F32, name="o_sb")
+            nc.scalar.copy(
+                out=o_sb[:, :, 1:4:2, :].rearrange("p s j d -> p j s d"),
+                in_=low[:].rearrange("p (j s) d -> p j s d", s=2),
+            )
+            flat = o_sb[:].rearrange("p s j d -> p (s j) d")
+            nc.scalar.copy(out=flat[:, 2:5:2, :], in_=high[:, 0:2, :])
+            nc.scalar.copy(out=flat[:, 0:7:6, :], in_=high[:, 2:4, :])
+            for s in range(2):
+                nc.sync.dma_start(out=out[2 * i + s, h].rearrange("(j p) d -> p j d", p=P), in_=o_sb[:, s])
 
         def live(n):
-            return 0 <= n < NH
+            return 0 <= n < NP
 
-        REGROUP = {2: (2,), 3: (2, 3), 0: (3,), 1: ()}
-
-        for it in range(-2, NH + 2):
-            if it >= 0 and it % H == 0 and it // H + AHEAD < B:
-                load(it // H + AHEAD)
+        for it in range(-2, NP + 2):
+            if it >= 0 and it % 2 == 0 and live(it + 6):
+                load(it + 6, it + 8)
             if live(it - 2):
                 second_matmul(it - 2)
             if live(it + 2):
                 transposes(it + 2)
-                if it + 2 < H:
-                    build_table(it + 2)
+            if it == -2:
+                for kind in ORDER:
+                    build_table(0, kind)
+            if it >= 0 and it % 4 < 3 and it // 4 + 1 < H:
+                for kind in (ORDER[0:2], ORDER[2:4], ORDER[4:5])[it % 4]:
+                    build_table(it // 4 + 1, kind)
+            if live(it):
+                regroup_v(it, 0)
+                regroup_v(it, 1)
             if live(it + 1):
-                scores(it + 1)
-                for ib in ON_G:
-                    feed(it + 1, ib)
-            for ahead in REGROUP[it % 4]:
-                if live(it + ahead):
-                    regroup_v(it + ahead)
+                for kind in ORDER:
+                    scores(it + 1, kind)
             if live(it):
-                decay(it, 2)
-                decay(it, 3)
-            if it % H == 1 and live(it):
-                quantise_v(it // H)
+                decay(it, "A3")
+                decay(it, "B3")
             if live(it - 1):
-                quantise_p(it - 1)
+                quantise_v(it - 1)
+                mask_values(it - 1)
+            if live(it + 2):
+                mask_keys(it + 2)
             if live(it):
-                decay(it, 1)
-                decay(it, 0)
+                decay(it, "X")
+                decay(it, "Y")
+            if live(it - 1):
+                quantise_p(it - 1, 0)
+            if live(it):
+                decay(it, "Z")
+            if live(it - 1):
+                quantise_p(it - 1, 1)

@@ -20,13 +20,7 @@ ACT = mybir.ActivationFunctionType
 
 FAR = 131072.0
 
-KINDS = {"A3": ((0, 3),), "B3": ((1, 3),), "X": ((0, 2), (1, 0)), "Y": ((1, 2), (0, 0)), "Z": ((0, 1), (1, 1))}
-ORDER = ("A3", "B3", "X", "Y", "Z")
-SLOT = {kind: i for i, kind in enumerate(ORDER)}
-
-
-def group_of(head, kg):
-    return kg if head == 0 else 3 - kg
+KINDS = (("A", 0), ("A", 1), ("B", 0), ("B", 1), ("L", 0), ("L", 1))
 
 
 def tile_model_pa_t_kernel(tc, q_scaled, k, v, out):
@@ -49,18 +43,27 @@ def tile_model_pa_t_kernel(tc, q_scaled, k, v, out):
             h, i0 = divmod(n0, 4)
             i1 = i0 + n1 - n0
             ni = n1 - n0
-            q_sb = inp.tile([P, 2 * ni, 4 * D], BF16, name="q_sb%d" % n0)
+            q_sb = inp.tile([P, 2 * ni, 2, 2 * D], BF16, name="q_sb%d" % n0)
             k_sb = inp.tile([P, 2, ni, 4 * D], BF16, name="k_sb%d" % n0)
             v_sb = inp.tile([P, 2, ni, 4 * D], BF16, name="v_sb%d" % n0)
-            nc.sync.dma_start(out=q_sb[:], in_=q_scaled[2 * i0 : 2 * i1, h].rearrange("b (m u) d -> m b (u d)", u=4))
-            for dst, src in ((k_sb, k_by_side), (v_sb, v_by_side)):
+
+            def keys(dst, src):
                 nc.sync.dma_start(out=dst[:, 0], in_=src[0, h, i0:i1].rearrange("i (p t) d -> p i (t d)", t=4))
-                for kg in range(4):
-                    g = group_of(1, kg)
+                for half in range(2):
                     nc.sync.dma_start(
-                        out=dst[32 * g : 32 * g + 32, 1],
-                        in_=src[1, h, i0:i1, 128 * kg : 128 * kg + 128].rearrange("i (p t) d -> p i (t d)", t=4),
+                        out=dst[64 - 64 * half : 128 - 64 * half, 1],
+                        in_=src[1, h, i0:i1, 256 * half : 256 * half + 256].rearrange("i (p t) d -> p i (t d)", t=4),
                     )
+
+            keys(k_sb, k_by_side)
+            for half in range(2):
+                nc.sync.dma_start(
+                    out=q_sb[:, :, half, :],
+                    in_=q_scaled[2 * i0 : 2 * i1, h, 256 * half : 256 * half + 256].rearrange(
+                        "b (m u) d -> m b (u d)", u=2
+                    ),
+                )
+            keys(v_sb, v_by_side)
             for j in range(ni):
                 place[n0 + j] = (q_sb, k_sb, v_sb, j)
 
@@ -68,57 +71,58 @@ def tile_model_pa_t_kernel(tc, q_scaled, k, v, out):
         for n0, n1 in GROUPS[:4]:
             load(n0, n1)
 
-        shift = const.tile([P, 5], F32, name="shift")
-        for kind in ORDER:
-            vals = [0] * 4
-            for head, qb in KINDS[kind]:
-                for kg in range(qb + 1):
-                    g = group_of(head, kg)
-                    vals[g] = float(128 * (g + qb - kg))
-            col = shift[:, SLOT[kind] : SLOT[kind] + 1]
-            for g in range(4):
-                nc.vector.memset(col[32 * g : 32 * g + 32, :], vals[g])
-
         ident = const.tile([P, P], BF16, name="ident")
         make_identity(nc, ident[:])
         expo0 = const.tile([P, 512], F32, name="expo0")
         nc.gpsimd.iota(
-            expo0[:], pattern=[[1, 128], [-1, 4]], base=0, channel_multiplier=-4, allow_small_or_imprecise_dtypes=True
+            expo0[:], pattern=[[2, 128], [-1, 4]], base=0, channel_multiplier=-4, allow_small_or_imprecise_dtypes=True
         )
-        expo = const.tile([P, 5, 512], F32, name="expo")
-        for kind in ORDER:
-            i = SLOT[kind]
+        shift = const.tile([P, 6], F32, name="shift")
+        for i, (side, u) in enumerate(KINDS):
+            low, high = {"A": (256, 256), "B": (0, 512), "L": (0, 256)}[side]
+            nc.vector.memset(shift[0:64, i : i + 1], float(low + u))
+            nc.vector.memset(shift[64:128, i : i + 1], float(high + u))
+        expo = const.tile([P, 6, 512], F32, name="expo")
+        for i in range(6):
             behind = work.tile([P, 512], F32, name="behind")
             nc.vector.tensor_scalar(
                 out=behind[:], in0=expo0[:], scalar1=shift[:, i : i + 1], scalar2=0.0, op0=ALU.add, op1=ALU.is_lt
             )
-            ahead = work.tile([P, 512], F32, name="ahead")
-            nc.vector.tensor_scalar_add(out=ahead[:], in0=expo0[:], scalar1=shift[:, i : i + 1])
             nc.vector.scalar_tensor_tensor(
-                out=expo[:, i, :], in0=behind[:], scalar=FAR, in1=ahead[:], op0=ALU.mult, op1=ALU.max
+                out=expo[:, i, :], in0=behind[:], scalar=FAR, in1=expo0[:], op0=ALU.mult, op1=ALU.add
             )
+            if i == 0:
+                offsets = []
+                for h in range(H):
+                    off = const.tile([P, 6], F32, name="off%d" % h)
+                    nc.vector.tensor_scalar_mul(out=off[:], in0=shift[:], scalar1=math.log(1.0 - 2.0 ** (-5 - h)))
+                    offsets.append(off)
         tabs = {}
 
-        def build_table(h, kind):
-            i = SLOT[kind]
+        def build_table(h, i):
             if i == 0:
-                tab = const.tile([P, 5, 512], F32, name="tab%d" % h)
+                tab = const.tile([P, 6, 512], F32, name="tab%d" % h)
                 tabs[h] = tab
             nc.scalar.activation(
-                out=tabs[h][:, i, :], in_=expo[:, i, :], func=ACT.Exp, scale=math.log(1.0 - 2.0 ** (-5 - h))
+                out=tabs[h][:, i, :],
+                in_=expo[:, i, :],
+                func=ACT.Exp,
+                scale=math.log(1.0 - 2.0 ** (-5 - h)),
+                bias=offsets[h][:, i : i + 1],
             )
 
         kz, vp, vz = [], [], []
         for i in range(2):
             for s in range(2):
-                t = const.tile([P, 4, 4, 128], BF16, name="kz%d%d" % (i, s))
-                nc.gpsimd.memset(t[:, 1:4].rearrange("p v t c -> p (v t c)").bitcast(I32), 0)
+                t = const.tile([P, 2, 4, 128], BF16, name="kz%d%d" % (i, s))
+                nc.gpsimd.memset(t[:, 1].rearrange("p t c -> p (t c)").bitcast(I32), 0)
                 kz.append(t)
-            p_full = const.tile([P, 2, 128], U8, name="vp%d" % i, align_bytes=64)
-            nc.vector.memset(p_full[:].rearrange("p s c -> p (s c)").bitcast(I32), 0)
+        for i in range(2):
+            p_full = const.tile([P, 2, 2, 128], U8, name="vp%d" % i, align_bytes=64)
+            nc.gpsimd.memset(p_full[:].rearrange("p n s c -> p (n s c)").bitcast(I32), 0)
             vp.append(p_full)
-            p_part = const.tile([P, 3, 2, 128], U8, name="vz%d" % i, align_bytes=64)
-            nc.gpsimd.memset(p_part[:].rearrange("p k s c -> p (k s c)").bitcast(I32), 0)
+            p_part = const.tile([P, 2, 2, 128], U8, name="vz%d" % i, align_bytes=64)
+            nc.gpsimd.memset(p_part[:].rearrange("p n s c -> p (n s c)").bitcast(I32), 0)
             vz.append(p_part)
 
         qT, s_ps, grouped, words, planes, vgs, vwords = {}, {}, {}, {}, {}, {}, {}
@@ -131,122 +135,114 @@ def tile_model_pa_t_kernel(tc, q_scaled, k, v, out):
                     nc.tensor.transpose(
                         t_ps[:, 128 * t : 128 * t + 128], k_sb[:, s, j, 128 * t : 128 * t + 128], ident[:]
                     )
-                for u in range(4):
-                    nc.tensor.transpose(
-                        t_ps[:, 512 + 128 * u : 640 + 128 * u], q_sb[:, 2 * j + s, 128 * u : 128 * u + 128], ident[:]
-                    )
-                nc.scalar.copy(out=kz[2 * (n % 2) + s][:, 0].rearrange("p t c -> p (t c)"), in_=t_ps[:, 0:512])
-                q_t = work.tile([P, 512], BF16, name="q_t%d" % s)
-                nc.scalar.copy(out=q_t[:], in_=t_ps[:, 512:1024])
+                for half in range(2):
+                    for u in range(2):
+                        slot = 512 + 128 * (2 * half + u)
+                        nc.tensor.transpose(
+                            t_ps[:, slot : slot + 128], q_sb[:, 2 * j + s, half, 128 * u : 128 * u + 128], ident[:]
+                        )
+                t_kz = kz[2 * (n % 2) + s]
+                nc.scalar.copy(out=t_kz[:, 0].rearrange("p t c -> p (t c)"), in_=t_ps[:, 0:512])
+                q_t = work.tile([P, 4, 128], BF16, name="q_t%d" % s)
+                nc.scalar.copy(out=q_t[:].rearrange("p j c -> p (j c)"), in_=t_ps[:, 512:1024])
+                low = slice(64 * s, 64 * s + 64)
+                nc.scalar.copy(
+                    out=t_kz[:, 1, :, low], in_=t_ps[:, 0:512].rearrange("p (t c) -> p t c", t=4)[:, :, low]
+                )
                 qT[(n, s)] = q_t
 
-        def mask_keys(n):
-            for s in range(2):
-                t = kz[2 * (n % 2) + s]
-                for z in range(1, 4):
-                    cols = slice(0, 128 - 32 * z) if s == 0 else slice(32 * z, 128)
-                    nc.gpsimd.tensor_copy(out=t[:, z, :, cols], in_=t[:, 0, :, cols])
-
-        def scores(n, kind):
+        def scores(n, i):
+            side, u = KINDS[i]
             s_tile = ps.tile([P, 4, 128], F32, name="s_ps")
-            s_ps[(n, kind)] = s_tile
-            parts = KINDS[kind]
+            s_ps[(n, i)] = s_tile
+            heads = {"A": (0,), "B": (1,), "L": (0, 1)}[side]
             for t in range(4):
-                for i, (head, qb) in enumerate(parts):
+                for head in heads:
                     nc.tensor.matmul(
-                        out=s_tile[:, t, :].rearrange("p (u m) -> p u m", u=4),
-                        lhsT=kz[2 * (n % 2) + head][:, 3 - qb, t, :],
-                        rhs=qT[(n, head)][:].rearrange("d (u m) -> d u m", u=4)[:, :, 32 * qb : 32 * qb + 32],
-                        start=i == 0,
-                        stop=i == len(parts) - 1,
+                        out=s_tile[:, t, :],
+                        lhsT=kz[2 * (n % 2) + head][:, 1 if side == "L" else 0, t, :],
+                        rhs=qT[(n, head)][:, u if side == "L" else 2 + u, :],
+                        start=head == heads[0],
+                        stop=head == heads[-1],
                     )
 
-        def decay(n, kind):
-            i = SLOT[kind]
+        def decay(n, i):
             if i == 0:
-                g_new = work.tile([P, 5, 512], BF16, name="grouped", align_bytes=64, bufs=2)
+                g_new = work.tile([P, 6, 512], BF16, name="grouped", align_bytes=64, bufs=2)
                 grouped[n] = g_new
             nc.vector.tensor_tensor(
-                out=grouped[n][:, i, :].rearrange("p (m u t) -> p m u t", u=4, t=4),
-                in0=s_ps[(n, kind)][:].rearrange("p t (u m) -> p m u t", u=4),
-                in1=tabs[n // 4][:, i, :].rearrange("p (m u t) -> p m u t", u=4, t=4),
+                out=grouped[n][:, i, :].rearrange("p (c t) -> p c t", t=4),
+                in0=s_ps[(n, i)][:].rearrange("p t c -> p c t"),
+                in1=tabs[n // 4][:, i, :].rearrange("p (c t) -> p c t", t=4),
                 op=ALU.mult,
             )
 
-        def quantise_p(n, part):
-            if part == 0:
-                w_new = work.tile([P, 5, 128], U32, name="w", align_bytes=64)
-                pl_new = work.tile([P, 5, 128], U8, name="pl", align_bytes=64)
-                words[n], planes[n] = w_new, pl_new
-            sel = slice(0, 4) if part == 0 else slice(4, 5)
-            nc.vector.quantize_mx(
-                out=words[n][:, sel, :].rearrange("p k c -> p (k c)").bitcast(FP8X4),
-                scales=planes[n][:, sel, :].rearrange("p k c -> p (k c)"),
-                in_=grouped[n][:, sel, :].rearrange("p k c -> p (k c)"),
-            )
+        def quantise_p(n):
+            w = work.tile([P, 6, 128], U32, name="w", align_bytes=64)
+            pl = work.tile([P, 6, 128], U8, name="pl", align_bytes=64)
+            words[n], planes[n] = w, pl
+            for sel in (slice(0, 4), slice(4, 6)):
+                nc.vector.quantize_mx(
+                    out=w[:, sel, :].rearrange("p k c -> p (k c)").bitcast(FP8X4),
+                    scales=pl[:, sel, :].rearrange("p k c -> p (k c)"),
+                    in_=grouped[n][:, sel, :].rearrange("p k c -> p (k c)"),
+                )
 
-        def regroup_v(n, s):
+        def regroup_v(n):
             q_sb, k_sb, v_sb, j = place[n]
-            if s == 0:
-                vg_new = work.tile([P, 2, 512], BF16, name="vg", align_bytes=64, bufs=2)
-                vgs[n] = vg_new
-            nc.scalar.copy(
-                out=vgs[n][:, s, :].rearrange("p (c i t) -> p c t i", i=4, t=4),
-                in_=v_sb[:, s, j, :].rearrange("p (t c i) -> p c t i", t=4, i=4),
-            )
+            if n % 2 == 0:
+                vg_new = work.tile([P, 2, 2, 512], BF16, name="vg", align_bytes=64, bufs=2)
+                vgs[n // 2] = vg_new
+            for s in range(2):
+                nc.scalar.copy(
+                    out=vgs[n // 2][:, n % 2, s, :].rearrange("p (c i t) -> p c t i", i=4, t=4),
+                    in_=v_sb[:, s, j, :].rearrange("p (t c i) -> p c t i", t=4, i=4),
+                )
 
-        def quantise_v(n):
-            vw = work.tile([P, 2, 128], U32, name="vw", align_bytes=64)
-            vwords[n] = vw
+        def quantise_v(m):
+            vw = work.tile([P, 2, 2, 128], U32, name="vw", align_bytes=64)
+            vwords[m] = vw
+            full, part = vp[m % 2], vz[m % 2]
             nc.vector.quantize_mx(
-                out=vw[:].rearrange("p s c -> p (s c)").bitcast(FP8X4),
-                scales=vp[n % 2][:].rearrange("p s c -> p (s c)"),
-                in_=vgs[n][:].rearrange("p s c -> p (s c)"),
+                out=vw[:].rearrange("p n s c -> p (n s c)").bitcast(FP8X4),
+                scales=full[:].rearrange("p n s c -> p (n s c)"),
+                in_=vgs[m][:].rearrange("p n s c -> p (n s c)"),
             )
 
-        def mask_values(n):
-            full, part = vp[n % 2], vz[n % 2]
-            for i, kind in enumerate(("X", "Y", "Z")):
-                for head, qb in KINDS[kind]:
-                    lo, hi = (0, 32 * qb + 32) if head == 0 else (96 - 32 * qb, 128)
-                    cuts = [(lo, hi)] if (lo, hi) != (32, 128) else [(32, 64), (64, 128)]
-                    for a, b in cuts:
-                        nc.gpsimd.tensor_copy(
-                            out=part[a:b, i, head, :].bitcast(I32), in_=full[a:b, head, :].bitcast(I32)
-                        )
+        def mask_values(m):
+            full, part = vp[m % 2], vz[m % 2]
+            for s in range(2):
+                rows = slice(64 * s, 64 * s + 64)
+                nc.vector.tensor_copy(out=part[rows, :, s, :].bitcast(I32), in_=full[rows, :, s, :].bitcast(I32))
 
         def second_matmul(n):
             h, i = divmod(n, 4)
-            low = po.tile([P, 4, 128], F32, name="o_low")
-            high = po.tile([P, 4, 128], F32, name="o_high")
-
-            def multiply(dst, kind, rhs, rhs_scale):
+            vw, full, part = vwords[n // 2], vp[n // 2 % 2], vz[n // 2 % 2]
+            high = po.tile([P, 2, 2, 128], F32, name="o_high")
+            low = po.tile([P, 2, 2, 128], F32, name="o_low")
+            for j, (side, u) in enumerate(KINDS):
+                heads = {"A": slice(0, 1), "B": slice(1, 2), "L": slice(0, 2)}[side]
+                dst = low[:, u, :, :] if side == "L" else high[:, heads, u, :]
+                scales = part if side == "L" else full
                 nc.tensor.matmul_mx(
-                    out=dst.rearrange("p j d -> p (j d)"),
-                    lhsT=words[n][:, SLOT[kind], :].bitcast(FP8X4),
-                    lhsT_scale=planes[n][:, SLOT[kind], :],
-                    rhs=rhs.rearrange("p s c -> p (s c)").bitcast(FP8X4),
-                    rhs_scale=rhs_scale.rearrange("p s c -> p (s c)"),
+                    out=dst.rearrange("p s d -> p (s d)"),
+                    lhsT=words[n][:, j, :].bitcast(FP8X4),
+                    lhsT_scale=planes[n][:, j, :],
+                    rhs=vw[:, n % 2, heads, :].rearrange("p s c -> p (s c)").bitcast(FP8X4),
+                    rhs_scale=scales[:, n % 2, heads, :].rearrange("p s c -> p (s c)"),
                     start=True,
                     stop=True,
                 )
-
-            vw = vwords[n]
-            multiply(low[:, 2:3, :], "A3", vw[:, 0:1, :], vp[n % 2][:, 0:1, :])
-            multiply(low[:, 3:4, :], "B3", vw[:, 1:2, :], vp[n % 2][:, 1:2, :])
-            multiply(low[:, 0:2, :], "Z", vw[:], vz[n % 2][:, 2])
-            multiply(high[:, 0:2, :], "X", vw[:], vz[n % 2][:, 0])
-            multiply(high[:, 2:4, :], "Y", vw[:], vz[n % 2][:, 1])
-            o_sb = outp.tile([P, 2, 4, 128], F32, name="o_sb")
+            o_sb = outp.tile([P, 2, 2, 2, 128], F32, name="o_sb")
             nc.scalar.copy(
-                out=o_sb[:, :, 1:4:2, :].rearrange("p s j d -> p j s d"),
-                in_=low[:].rearrange("p (j s) d -> p j s d", s=2),
+                out=o_sb[:, :, 1].rearrange("p s u d -> p s (u d)"), in_=high[:].rearrange("p s u d -> p s (u d)")
             )
-            flat = o_sb[:].rearrange("p s j d -> p (s j) d")
-            nc.scalar.copy(out=flat[:, 2:5:2, :], in_=high[:, 0:2, :])
-            nc.scalar.copy(out=flat[:, 0:7:6, :], in_=high[:, 2:4, :])
+            nc.scalar.copy(out=o_sb[:, :, 0].rearrange("p s u d -> p u s d"), in_=low[:])
             for s in range(2):
-                nc.sync.dma_start(out=out[2 * i + s, h].rearrange("(j p) d -> p j d", p=P), in_=o_sb[:, s])
+                nc.sync.dma_start(
+                    out=out[2 * i + s, h].rearrange("(f m u) d -> m f (u d)", f=2, u=2),
+                    in_=o_sb[:, s].rearrange("p f u d -> p f (u d)"),
+                )
 
         def live(n):
             return 0 <= n < NP
@@ -259,31 +255,28 @@ def tile_model_pa_t_kernel(tc, q_scaled, k, v, out):
             if live(it + 2):
                 transposes(it + 2)
             if it == -2:
-                for kind in ORDER:
-                    build_table(0, kind)
-            if it >= 0 and it % 4 < 3 and it // 4 + 1 < H:
-                for kind in (ORDER[0:2], ORDER[2:4], ORDER[4:5])[it % 4]:
-                    build_table(it // 4 + 1, kind)
-            if live(it):
-                regroup_v(it, 0)
-                regroup_v(it, 1)
+                for i in range(6):
+                    build_table(0, i)
             if live(it + 1):
-                for kind in ORDER:
-                    scores(it + 1, kind)
+                regroup_v(it + 1)
+            if it >= 0 and it // 4 + 1 < H:
+                for i in ((0, 1), (2, 3), (4,), (5,))[it % 4]:
+                    build_table(it // 4 + 1, i)
+            if live(it + 1):
+                for i in range(6):
+                    scores(it + 1, i)
             if live(it):
-                decay(it, "A3")
-                decay(it, "B3")
+                decay(it, 0)
+                decay(it, 1)
             if live(it - 1):
-                quantise_v(it - 1)
-                mask_values(it - 1)
-            if live(it + 2):
-                mask_keys(it + 2)
+                quantise_p(it - 1)
+            if live(it) and it % 2 == 1:
+                quantise_v(it // 2)
             if live(it):
-                decay(it, "X")
-                decay(it, "Y")
-            if live(it - 1):
-                quantise_p(it - 1, 0)
+                decay(it, 2)
+                decay(it, 3)
+            if live(it) and it % 2 == 1:
+                mask_values(it // 2)
             if live(it):
-                decay(it, "Z")
-            if live(it - 1):
-                quantise_p(it - 1, 1)
+                decay(it, 4)
+                decay(it, 5)

@@ -83,20 +83,21 @@ def tile_model_pa_t_kernel(tc, q_scaled, k, v, out):
             nc.vector.memset(shift[0:64, i : i + 1], float(low + u))
             nc.vector.memset(shift[64:128, i : i + 1], float(high + u))
         expo = const.tile([P, 6, 512], F32, name="expo")
-        for i in range(6):
-            behind = work.tile([P, 512], F32, name="behind")
+        offsets = []
+        for h in range(H):
+            off = const.tile([P, 6], F32, name="off%d" % h)
+            nc.vector.tensor_scalar_mul(out=off[:], in0=shift[:], scalar1=math.log(1.0 - 2.0 ** (-5 - h)))
+            offsets.append(off)
+
+        def build_exponents(i):
+            behind = work.tile([P, 512], F32, name="behind", bufs=2)
             nc.vector.tensor_scalar(
                 out=behind[:], in0=expo0[:], scalar1=shift[:, i : i + 1], scalar2=0.0, op0=ALU.add, op1=ALU.is_lt
             )
             nc.vector.scalar_tensor_tensor(
                 out=expo[:, i, :], in0=behind[:], scalar=FAR, in1=expo0[:], op0=ALU.mult, op1=ALU.add
             )
-            if i == 0:
-                offsets = []
-                for h in range(H):
-                    off = const.tile([P, 6], F32, name="off%d" % h)
-                    nc.vector.tensor_scalar_mul(out=off[:], in0=shift[:], scalar1=math.log(1.0 - 2.0 ** (-5 - h)))
-                    offsets.append(off)
+
         tabs = {}
 
         def build_table(h, i):
@@ -125,31 +126,33 @@ def tile_model_pa_t_kernel(tc, q_scaled, k, v, out):
             nc.gpsimd.memset(p_part[:].rearrange("p n s c -> p (n s c)").bitcast(I32), 0)
             vz.append(p_part)
 
-        qT, s_ps, grouped, words, planes, vgs, vwords = {}, {}, {}, {}, {}, {}, {}
+        qT, s_ps, fed, upper, lower, words, planes, vgs, vwords = {}, {}, {}, {}, {}, {}, {}, {}, {}
 
-        def transposes(n):
+        def transposes(n, s):
             q_sb, k_sb, v_sb, j = place[n]
-            for s in range(2):
-                t_ps = pt.tile([P, 1024], BF16, name="t_ps")
-                for t in range(4):
-                    nc.tensor.transpose(
-                        t_ps[:, 128 * t : 128 * t + 128], k_sb[:, s, j, 128 * t : 128 * t + 128], ident[:]
-                    )
-                for half in range(2):
-                    for u in range(2):
-                        slot = 512 + 128 * (2 * half + u)
-                        nc.tensor.transpose(
-                            t_ps[:, slot : slot + 128], q_sb[:, 2 * j + s, half, 128 * u : 128 * u + 128], ident[:]
-                        )
-                t_kz = kz[2 * (n % 2) + s]
-                nc.scalar.copy(out=t_kz[:, 0].rearrange("p t c -> p (t c)"), in_=t_ps[:, 0:512])
-                q_t = work.tile([P, 4, 128], BF16, name="q_t%d" % s)
-                nc.scalar.copy(out=q_t[:].rearrange("p j c -> p (j c)"), in_=t_ps[:, 512:1024])
-                low = slice(64 * s, 64 * s + 64)
-                nc.scalar.copy(
-                    out=t_kz[:, 1, :, low], in_=t_ps[:, 0:512].rearrange("p (t c) -> p t c", t=4)[:, :, low]
+            t_ps = pt.tile([P, 1024], BF16, name="t_ps")
+            for t in range(4):
+                nc.tensor.transpose(
+                    t_ps[:, 128 * t : 128 * t + 128], k_sb[:, s, j, 128 * t : 128 * t + 128], ident[:]
                 )
-                qT[(n, s)] = q_t
+            for half in range(2):
+                for u in range(2):
+                    slot = 512 + 128 * (2 * half + u)
+                    nc.tensor.transpose(
+                        t_ps[:, slot : slot + 128], q_sb[:, 2 * j + s, half, 128 * u : 128 * u + 128], ident[:]
+                    )
+            t_kz = kz[2 * (n % 2) + s]
+            t_words = t_ps[:].bitcast(F32)
+            k_words = t_kz[:].rearrange("p z t c -> p (z t c)").bitcast(F32)
+            nc.scalar.copy(out=k_words[:, 0:256], in_=t_words[:, 0:256])
+            q_t = work.tile([P, 512], BF16, name="q_t%d" % s)
+            nc.scalar.copy(out=q_t[:].bitcast(F32), in_=t_words[:, 256:512])
+            low = slice(32 * s, 32 * s + 32)
+            nc.scalar.copy(
+                out=k_words[:, 256:512].rearrange("p (t c) -> p t c", t=4)[:, :, low],
+                in_=t_words[:, 0:256].rearrange("p (t c) -> p t c", t=4)[:, :, low],
+            )
+            qT[(n, s)] = q_t
 
         def scores(n, i):
             side, u = KINDS[i]
@@ -161,43 +164,57 @@ def tile_model_pa_t_kernel(tc, q_scaled, k, v, out):
                     nc.tensor.matmul(
                         out=s_tile[:, t, :],
                         lhsT=kz[2 * (n % 2) + head][:, 1 if side == "L" else 0, t, :],
-                        rhs=qT[(n, head)][:, u if side == "L" else 2 + u, :],
+                        rhs=qT[(n, head)][:, slice(128 * u, 128 * u + 128) if side == "L" else slice(256 + 128 * u, 384 + 128 * u)],
                         start=head == heads[0],
                         stop=head == heads[-1],
                     )
 
+        def feed(n):
+            f = work.tile([P, 512], F32, name="fed", bufs=2)
+            fed[n] = f
+            nc.scalar.copy(
+                out=f[:].rearrange("p (c t) -> p c t", t=4), in_=s_ps[(n, 5)][:].rearrange("p t c -> p c t")
+            )
+
+        def decay_fed(n):
+            nc.gpsimd.tensor_tensor(out=lower[n][:, 1, :], in0=fed[n][:], in1=tabs[n // 4][:, 5, :], op=ALU.mult)
+
         def decay(n, i):
             if i == 0:
-                g_new = work.tile([P, 6, 512], BF16, name="grouped", align_bytes=64, bufs=2)
-                grouped[n] = g_new
+                u_new = work.tile([P, 4, 512], BF16, name="upper", align_bytes=64, bufs=2)
+                upper[n] = u_new
+            dst = upper[n][:, i, :] if i < 4 else lower[n][:, i - 4, :]
             nc.vector.tensor_tensor(
-                out=grouped[n][:, i, :].rearrange("p (c t) -> p c t", t=4),
+                out=dst.rearrange("p (c t) -> p c t", t=4),
                 in0=s_ps[(n, i)][:].rearrange("p t c -> p c t"),
                 in1=tabs[n // 4][:, i, :].rearrange("p (c t) -> p c t", t=4),
                 op=ALU.mult,
             )
 
-        def quantise_p(n):
-            w = work.tile([P, 6, 128], U32, name="w", align_bytes=64)
-            pl = work.tile([P, 6, 128], U8, name="pl", align_bytes=64)
-            words[n], planes[n] = w, pl
-            for sel in (slice(0, 4), slice(4, 6)):
-                nc.vector.quantize_mx(
-                    out=w[:, sel, :].rearrange("p k c -> p (k c)").bitcast(FP8X4),
-                    scales=pl[:, sel, :].rearrange("p k c -> p (k c)"),
-                    in_=grouped[n][:, sel, :].rearrange("p k c -> p (k c)"),
-                )
+        def new_lower(n):
+            l_new = work.tile([P, 2, 512], BF16, name="lower", align_bytes=64, bufs=1)
+            lower[n] = l_new
+
+        def quantise_p(n, sel):
+            if sel.start == 0:
+                w_new = work.tile([P, 6, 128], U32, name="w", align_bytes=64)
+                pl_new = work.tile([P, 6, 128], U8, name="pl", align_bytes=64)
+                words[n], planes[n] = w_new, pl_new
+            nc.vector.quantize_mx(
+                out=words[n][:, sel, :].rearrange("p k c -> p (k c)").bitcast(FP8X4),
+                scales=planes[n][:, sel, :].rearrange("p k c -> p (k c)"),
+                in_=(upper if sel.start == 0 else lower)[n][:].rearrange("p k c -> p (k c)"),
+            )
 
         def regroup_v(n):
             q_sb, k_sb, v_sb, j = place[n]
             if n % 2 == 0:
                 vg_new = work.tile([P, 2, 2, 512], BF16, name="vg", align_bytes=64, bufs=2)
                 vgs[n // 2] = vg_new
-            for s in range(2):
-                nc.scalar.copy(
-                    out=vgs[n // 2][:, n % 2, s, :].rearrange("p (c i t) -> p c t i", i=4, t=4),
-                    in_=v_sb[:, s, j, :].rearrange("p (t c i) -> p c t i", t=4, i=4),
-                )
+            nc.gpsimd.tensor_copy(
+                out=vgs[n // 2][:, n % 2].rearrange("p s (c t) -> p s c t", t=4),
+                in_=v_sb[:, :, j, :].rearrange("p s (t c) -> p s c t", t=4),
+            )
 
         def quantise_v(m):
             vw = work.tile([P, 2, 2, 128], U32, name="vw", align_bytes=64)
@@ -213,7 +230,7 @@ def tile_model_pa_t_kernel(tc, q_scaled, k, v, out):
             full, part = vp[m % 2], vz[m % 2]
             for s in range(2):
                 rows = slice(64 * s, 64 * s + 64)
-                nc.vector.tensor_copy(out=part[rows, :, s, :].bitcast(I32), in_=full[rows, :, s, :].bitcast(I32))
+                nc.gpsimd.tensor_copy(out=part[rows, :, s, :].bitcast(I32), in_=full[rows, :, s, :].bitcast(I32))
 
         def second_matmul(n):
             h, i = divmod(n, 4)
@@ -237,7 +254,8 @@ def tile_model_pa_t_kernel(tc, q_scaled, k, v, out):
             nc.scalar.copy(
                 out=o_sb[:, :, 1].rearrange("p s u d -> p s (u d)"), in_=high[:].rearrange("p s u d -> p s (u d)")
             )
-            nc.scalar.copy(out=o_sb[:, :, 0].rearrange("p s u d -> p u s d"), in_=low[:])
+            copy_low = nc.vector.tensor_copy if n == NP - 1 else nc.scalar.copy
+            copy_low(out=o_sb[:, :, 0].rearrange("p s u d -> p u s d"), in_=low[:])
             for s in range(2):
                 nc.sync.dma_start(
                     out=out[2 * i + s, h].rearrange("(f m u) d -> m f (u d)", f=2, u=2),
@@ -247,36 +265,58 @@ def tile_model_pa_t_kernel(tc, q_scaled, k, v, out):
         def live(n):
             return 0 <= n < NP
 
+        UPPER, LOWER = slice(0, 4), slice(4, 6)
+
         for it in range(-2, NP + 2):
             if it >= 0 and it % 2 == 0 and live(it + 6):
                 load(it + 6, it + 8)
+            if it == 0:
+                for i in range(2):
+                    decay(0, i)
+                    build_exponents(4 + i)
+                    build_table(0, 4 + i)
+                regroup_v(0)
+                regroup_v(1)
             if live(it - 2):
                 second_matmul(it - 2)
-            if live(it + 2):
-                transposes(it + 2)
             if it == -2:
-                for i in range(6):
+                transposes(0, 0)
+                transposes(0, 1)
+            if it == -2:
+                for i in range(4):
+                    build_exponents(i)
                     build_table(0, i)
-            if live(it + 1):
-                regroup_v(it + 1)
             if it >= 0 and it // 4 + 1 < H:
                 for i in ((0, 1), (2, 3), (4,), (5,))[it % 4]:
                     build_table(it // 4 + 1, i)
-            if live(it + 1):
-                for i in range(6):
+            for i in (0, 1, 5, 2, 3, 4):
+                if live(it + 1):
                     scores(it + 1, i)
-            if live(it):
+                    if i == 5:
+                        feed(it + 1)
+                if it > -2 and live(it + 2) and i in (1, 2):
+                    transposes(it + 2, i - 1)
+            if live(it) and it > 0:
                 decay(it, 0)
                 decay(it, 1)
-            if live(it - 1):
-                quantise_p(it - 1)
             if live(it) and it % 2 == 1:
                 quantise_v(it // 2)
+            if live(it - 1) and it < NP:
+                quantise_p(it - 1, UPPER)
+                quantise_p(it - 1, LOWER)
+            if live(it):
+                new_lower(it)
+                decay_fed(it)
+            if live(it) and it % 2 == 1:
+                mask_values(it // 2)
+            if it >= 0 and live(it + 2):
+                regroup_v(it + 2)
             if live(it):
                 decay(it, 2)
                 decay(it, 3)
-            if live(it) and it % 2 == 1:
-                mask_values(it // 2)
+            if it == NP - 1:
+                quantise_p(it, UPPER)
             if live(it):
                 decay(it, 4)
-                decay(it, 5)
+            if it == NP - 1:
+                quantise_p(it, LOWER)

@@ -211,9 +211,17 @@ def tile_model_pa_t_kernel(tc, q_scaled, k, v, out):
             if n % 2 == 0:
                 vg_new = work.tile([P, 2, 2, 512], BF16, name="vg", align_bytes=64, bufs=2)
                 vgs[n // 2] = vg_new
-            nc.gpsimd.tensor_copy(
-                out=vgs[n // 2][:, n % 2].rearrange("p s (c t) -> p s c t", t=4),
-                in_=v_sb[:, :, j, :].rearrange("p s (t c) -> p s c t", t=4),
+            nc.scalar.copy(
+                out=vgs[n // 2][:, n % 2, 0, :].rearrange("p (c i t) -> p c t i", i=4, t=4),
+                in_=v_sb[:, 0, j, :].rearrange("p (t c i) -> p c t i", t=4, i=4),
+            )
+            nc.gpsimd.tensor_scalar(
+                out=vgs[n // 2][:, n % 2, 1, :].rearrange("p (c t) -> p c t", t=4),
+                in0=v_sb[:, 1, j, :].rearrange("p (t c) -> p c t", t=4),
+                scalar1=1.0,
+                scalar2=0.0,
+                op0=ALU.mult,
+                op1=ALU.add,
             )
 
         def quantise_v(m):

import math
from contextlib import ExitStack

import concourse.mybir as mybir
from concourse.masks import make_identity

B, H, L, D = 8, 4, 512, 128
P = 128
NP = B * H // 2
FLOPS = 4 * B * H * L * L * D

BF16 = mybir.dt.bfloat16
F32 = mybir.dt.float32
I32 = mybir.dt.int32
U32 = mybir.dt.uint32
U8 = mybir.dt.uint8
FP8X4 = mybir.dt.float8_e4m3fn_x4
ALU = mybir.AluOpType
ACT = mybir.ActivationFunctionType

FAR = 131072.0

KINDS = (("A", 0), ("A", 1), ("B", 0), ("B", 1), ("L", 0), ("L", 1))


def tile_model_pa_t_kernel(tc, q_scaled, k, v, out):
    nc = tc.nc
    with ExitStack() as ctx:
        ctx.enter_context(tc.manual_schedule())
        const = ctx.enter_context(tc.tile_pool(name="const", bufs=1))
        inp = ctx.enter_context(tc.tile_pool(name="inp", bufs=1))
        work = ctx.enter_context(tc.tile_pool(name="work", bufs=3))
        outp = ctx.enter_context(tc.tile_pool(name="outp", bufs=3))
        pt = ctx.enter_context(tc.psum_pool(name="pt", bufs=2))
        ps = ctx.enter_context(tc.psum_pool(name="ps", bufs=4))
        po = ctx.enter_context(tc.psum_pool(name="po", bufs=1))

        k_by_side = k.rearrange("(i s) h l d -> s h i l d", s=2)
        v_by_side = v.rearrange("(i s) h l d -> s h i l d", s=2)
        place = {}

        def load(n0, n1):
            h, i0 = divmod(n0, 4)
            i1 = i0 + n1 - n0
            ni = n1 - n0
            q_sb = inp.tile([P, 2 * ni, 2, 2 * D], BF16, name="q_sb%d" % n0)
            k_sb = inp.tile([P, 2, ni, 4 * D], BF16, name="k_sb%d" % n0)
            v_sb = inp.tile([P, 2, ni, 4 * D], BF16, name="v_sb%d" % n0)

            def keys(dst, src):
                nc.sync.dma_start(out=dst[:, 0], in_=src[0, h, i0:i1].rearrange("i (p t) d -> p i (t d)", t=4))
                for half in range(2):
                    nc.sync.dma_start(
                        out=dst[64 - 64 * half : 128 - 64 * half, 1],
                        in_=src[1, h, i0:i1, 256 * half : 256 * half + 256].rearrange("i (p t) d -> p i (t d)", t=4),
                    )

            keys(k_sb, k_by_side)
            for half in range(2):
                nc.sync.dma_start(
                    out=q_sb[:, :, half, :],
                    in_=q_scaled[2 * i0 : 2 * i1, h, 256 * half : 256 * half + 256].rearrange(
                        "b (m u) d -> m b (u d)", u=2
                    ),
                )
            keys(v_sb, v_by_side)
            for j in range(ni):
                place[n0 + j] = (q_sb, k_sb, v_sb, j)

        GROUPS = [(0, 1), (1, 2), (2, 4)] + [(n, n + 2) for n in range(4, NP, 2)]
        for n0, n1 in GROUPS[:4]:
            load(n0, n1)

        ident = const.tile([P, P], BF16, name="ident")
        make_identity(nc, ident[:])
        expo0 = const.tile([P, 512], F32, name="expo0")
        nc.gpsimd.iota(
            expo0[:], pattern=[[2, 128], [-1, 4]], base=0, channel_multiplier=-4, allow_small_or_imprecise_dtypes=True
        )
        shift = const.tile([P, 6], F32, name="shift")
        for i, (side, u) in enumerate(KINDS):
            low, high = {"A": (256, 256), "B": (0, 512), "L": (0, 256)}[side]
            nc.vector.memset(shift[0:64, i : i + 1], float(low + u))
            nc.vector.memset(shift[64:128, i : i + 1], float(high + u))
        expo = const.tile([P, 6, 512], F32, name="expo")
        offsets = []
        for h in range(H):
            off = const.tile([P, 6], F32, name="off%d" % h)
            nc.vector.tensor_scalar_mul(out=off[:], in0=shift[:], scalar1=math.log(1.0 - 2.0 ** (-5 - h)))
            offsets.append(off)

        def build_exponents(i):
            behind = work.tile([P, 512], F32, name="behind", bufs=2)
            nc.vector.tensor_scalar(
                out=behind[:], in0=expo0[:], scalar1=shift[:, i : i + 1], scalar2=0.0, op0=ALU.add, op1=ALU.is_lt
            )
            nc.vector.scalar_tensor_tensor(
                out=expo[:, i, :], in0=behind[:], scalar=FAR, in1=expo0[:], op0=ALU.mult, op1=ALU.add
            )

        tabs = {}

        def build_table(h, i):
            if i == 0:
                tab = const.tile([P, 6, 512], F32, name="tab%d" % h)
                tabs[h] = tab
            nc.scalar.activation(
                out=tabs[h][:, i, :],
                in_=expo[:, i, :],
                func=ACT.Exp,
                scale=math.log(1.0 - 2.0 ** (-5 - h)),
                bias=offsets[h][:, i : i + 1],
            )

        kz, vp, vz = [], [], []
        for i in range(2):
            for s in range(2):
                t = const.tile([P, 2, 4, 128], BF16, name="kz%d%d" % (i, s))
                nc.gpsimd.memset(t[:, 1].rearrange("p t c -> p (t c)").bitcast(I32), 0)
                kz.append(t)
        for i in range(2):
            p_full = const.tile([P, 2, 2, 128], U8, name="vp%d" % i, align_bytes=64)
            nc.gpsimd.memset(p_full[:].rearrange("p n s c -> p (n s c)").bitcast(I32), 0)
            vp.append(p_full)
            p_part = const.tile([P, 2, 2, 128], U8, name="vz%d" % i, align_bytes=64)
            nc.gpsimd.memset(p_part[:].rearrange("p n s c -> p (n s c)").bitcast(I32), 0)
            vz.append(p_part)

        qT, s_ps, fed, upper, lower, words, planes, vgs, vwords = {}, {}, {}, {}, {}, {}, {}, {}, {}

        def transposes(n, s):
            q_sb, k_sb, v_sb, j = place[n]
            t_ps = pt.tile([P, 1024], BF16, name="t_ps")
            for t in range(4):
                nc.tensor.transpose(
                    t_ps[:, 128 * t : 128 * t + 128], k_sb[:, s, j, 128 * t : 128 * t + 128], ident[:]
                )
            for half in range(2):
                for u in range(2):
                    slot = 512 + 128 * (2 * half + u)
                    nc.tensor.transpose(
                        t_ps[:, slot : slot + 128], q_sb[:, 2 * j + s, half, 128 * u : 128 * u + 128], ident[:]
                    )
            t_kz = kz[2 * (n % 2) + s]
            t_words = t_ps[:].bitcast(F32)
            k_words = t_kz[:].rearrange("p z t c -> p (z t c)").bitcast(F32)
            nc.scalar.copy(out=k_words[:, 0:256], in_=t_words[:, 0:256])
            q_t = work.tile([P, 512], BF16, name="q_t%d" % s)
            nc.scalar.copy(out=q_t[:].bitcast(F32), in_=t_words[:, 256:512])
            low = slice(32 * s, 32 * s + 32)
            nc.scalar.copy(
                out=k_words[:, 256:512].rearrange("p (t c) -> p t c", t=4)[:, :, low],
                in_=t_words[:, 0:256].rearrange("p (t c) -> p t c", t=4)[:, :, low],
            )
            qT[(n, s)] = q_t

        def scores(n, i):
            side, u = KINDS[i]
            s_tile = ps.tile([P, 4, 128], F32, name="s_ps")
            s_ps[(n, i)] = s_tile
            heads = {"A": (0,), "B": (1,), "L": (0, 1)}[side]
            for t in range(4):
                for head in heads:
                    nc.tensor.matmul(
                        out=s_tile[:, t, :],
                        lhsT=kz[2 * (n % 2) + head][:, 1 if side == "L" else 0, t, :],
                        rhs=qT[(n, head)][:, slice(128 * u, 128 * u + 128) if side == "L" else slice(256 + 128 * u, 384 + 128 * u)],
                        start=head == heads[0],
                        stop=head == heads[-1],
                    )

        def feed(n):
            f = work.tile([P, 512], F32, name="fed", bufs=2)
            fed[n] = f
            nc.scalar.copy(
                out=f[:].rearrange("p (c t) -> p c t", t=4), in_=s_ps[(n, 5)][:].rearrange("p t c -> p c t")
            )

        def decay_fed(n):
            nc.gpsimd.tensor_tensor(out=lower[n][:, 1, :], in0=fed[n][:], in1=tabs[n // 4][:, 5, :], op=ALU.mult)

        def decay(n, i):
            if i == 0:
                u_new = work.tile([P, 4, 512], BF16, name="upper", align_bytes=64, bufs=2)
                upper[n] = u_new
            dst = upper[n][:, i, :] if i < 4 else lower[n][:, i - 4, :]
            nc.vector.tensor_tensor(
                out=dst.rearrange("p (c t) -> p c t", t=4),
                in0=s_ps[(n, i)][:].rearrange("p t c -> p c t"),
                in1=tabs[n // 4][:, i, :].rearrange("p (c t) -> p c t", t=4),
                op=ALU.mult,
            )

        def new_lower(n):
            l_new = work.tile([P, 2, 512], BF16, name="lower", align_bytes=64, bufs=1)
            lower[n] = l_new

        def quantise_p(n, sel):
            if sel.start == 0:
                w_new = work.tile([P, 6, 128], U32, name="w", align_bytes=64)
                pl_new = work.tile([P, 6, 128], U8, name="pl", align_bytes=64)
                words[n], planes[n] = w_new, pl_new
            nc.vector.quantize_mx(
                out=words[n][:, sel, :].rearrange("p k c -> p (k c)").bitcast(FP8X4),
                scales=planes[n][:, sel, :].rearrange("p k c -> p (k c)"),
                in_=(upper if sel.start == 0 else lower)[n][:].rearrange("p k c -> p (k c)"),
            )

        def regroup_v(n):
            q_sb, k_sb, v_sb, j = place[n]
            if n % 2 == 0:
                vg_new = work.tile([P, 2, 2, 512], BF16, name="vg", align_bytes=64, bufs=2)
                vgs[n // 2] = vg_new
            nc.scalar.copy(
                out=vgs[n // 2][:, n % 2, 0, :].rearrange("p (c i t) -> p c t i", i=4, t=4),
                in_=v_sb[:, 0, j, :].rearrange("p (t c i) -> p c t i", t=4, i=4),
            )
            nc.gpsimd.tensor_scalar(
                out=vgs[n // 2][:, n % 2, 1, :].rearrange("p (c t) -> p c t", t=4),
                in0=v_sb[:, 1, j, :].rearrange("p (t c) -> p c t", t=4),
                scalar1=1.0,
                scalar2=0.0,
                op0=ALU.mult,
                op1=ALU.add,
            )

        def quantise_v(m):
            vw = work.tile([P, 2, 2, 128], U32, name="vw", align_bytes=64)
            vwords[m] = vw
            full, part = vp[m % 2], vz[m % 2]
            nc.vector.quantize_mx(
                out=vw[:].rearrange("p n s c -> p (n s c)").bitcast(FP8X4),
                scales=full[:].rearrange("p n s c -> p (n s c)"),
                in_=vgs[m][:].rearrange("p n s c -> p (n s c)"),
            )

        def mask_values(m):
            full, part = vp[m % 2], vz[m % 2]
            for s in range(2):
                rows = slice(64 * s, 64 * s + 64)
                nc.gpsimd.tensor_copy(out=part[rows, :, s, :].bitcast(I32), in_=full[rows, :, s, :].bitcast(I32))

        def second_matmul(n):
            h, i = divmod(n, 4)
            vw, full, part = vwords[n // 2], vp[n // 2 % 2], vz[n // 2 % 2]
            high = po.tile([P, 2, 2, 128], F32, name="o_high")
            low = po.tile([P, 2, 2, 128], F32, name="o_low")
            for j, (side, u) in enumerate(KINDS):
                heads = {"A": slice(0, 1), "B": slice(1, 2), "L": slice(0, 2)}[side]
                dst = low[:, u, :, :] if side == "L" else high[:, heads, u, :]
                scales = part if side == "L" else full
                nc.tensor.matmul_mx(
                    out=dst.rearrange("p s d -> p (s d)"),
                    lhsT=words[n][:, j, :].bitcast(FP8X4),
                    lhsT_scale=planes[n][:, j, :],
                    rhs=vw[:, n % 2, heads, :].rearrange("p s c -> p (s c)").bitcast(FP8X4),
                    rhs_scale=scales[:, n % 2, heads, :].rearrange("p s c -> p (s c)"),
                    start=True,
                    stop=True,
                )
            o_sb = outp.tile([P, 2, 2, 2, 128], F32, name="o_sb")
            nc.scalar.copy(
                out=o_sb[:, :, 1].rearrange("p s u d -> p s (u d)"), in_=high[:].rearrange("p s u d -> p s (u d)")
            )
            copy_low = nc.vector.tensor_copy if n == NP - 1 else nc.scalar.copy
            copy_low(out=o_sb[:, :, 0].rearrange("p s u d -> p u s d"), in_=low[:])
            for s in range(2):
                nc.sync.dma_start(
                    out=out[2 * i + s, h].rearrange("(f m u) d -> m f (u d)", f=2, u=2),
                    in_=o_sb[:, s].rearrange("p f u d -> p f (u d)"),
                )

        def live(n):
            return 0 <= n < NP

        UPPER, LOWER = slice(0, 4), slice(4, 6)

        for it in range(-2, NP + 2):
            if it >= 0 and it % 2 == 0 and live(it + 6):
                load(it + 6, it + 8)
            if it == 0:
                for i in range(2):
                    decay(0, i)
                    build_exponents(4 + i)
                    build_table(0, 4 + i)
                regroup_v(0)
                regroup_v(1)
            if live(it - 2):
                second_matmul(it - 2)
            if it == -2:
                transposes(0, 0)
                transposes(0, 1)
            if it == -2:
                for i in range(4):
                    build_exponents(i)
                    build_table(0, i)
            if it >= 0 and it // 4 + 1 < H:
                for i in ((0, 1), (2, 3), (4,), (5,))[it % 4]:
                    build_table(it // 4 + 1, i)
            for i in (0, 1, 5, 2, 3, 4):
                if live(it + 1):
                    scores(it + 1, i)
                    if i == 5:
                        feed(it + 1)
                if it > -2 and live(it + 2) and i in (1, 2):
                    transposes(it + 2, i - 1)
            if live(it) and it > 0:
                decay(it, 0)
                decay(it, 1)
            if live(it) and it % 2 == 1:
                quantise_v(it // 2)
            if live(it - 1) and it < NP:
                quantise_p(it - 1, UPPER)
                quantise_p(it - 1, LOWER)
            if live(it):
                new_lower(it)
                decay_fed(it)
            if live(it) and it % 2 == 1:
                mask_values(it // 2)
            if it >= 0 and live(it + 2):
                regroup_v(it + 2)
            if live(it):
                decay(it, 2)
                decay(it, 3)
            if it == NP - 1:
                quantise_p(it, UPPER)
            if live(it):
                decay(it, 4)
            if it == NP - 1:
                quantise_p(it, LOWER)
